import numpy as np
import ml_dtypes


def mxq(x, axis, fmt="e4m3"):
    dtype, down = {"e4m3": (ml_dtypes.float8_e4m3fn, 7), "e5m2": (ml_dtypes.float8_e5m2, 14)}[fmt]
    v = np.moveaxis(np.asarray(x, np.float32).astype(ml_dtypes.bfloat16).astype(np.float64), axis, -1)
    blocks = v.reshape(v.shape[:-1] + (-1, 32))
    amax = np.abs(blocks).max(-1, keepdims=True)
    byte = np.maximum(np.where(amax > 0, np.frexp(amax)[1] - 1 + 127, 0) - down, 1)
    scale = np.exp2(byte - 127.0)
    codes = (blocks / scale).astype(np.float32).astype(dtype).astype(np.float64)
    return np.moveaxis((codes * scale).reshape(v.shape), -1, axis)


WIDE = False


def mx_kscale(k):
    if not WIDE:
        return np.ones(k)
    levels = np.array([10, -10, 5, -5, 0])
    if k % 512:
        return np.exp2(np.random.permutation(np.resize(levels, k // 32))).repeat(32)
    a = np.empty((k // 512, 16))
    for p in range(k // 512):
        a[p, :8] = np.random.permutation(np.resize(levels, 8))
        for g in range(8):
            far = levels[np.abs(levels - a[p, g]) >= 10]
            a[p, g + 8] = far[np.random.randint(len(far))]
    return np.exp2(a.ravel()).repeat(32)


BF16 = ml_dtypes.bfloat16


def bf(x):
    return np.asarray(x, np.float32).astype(BF16)


def f64(x):
    return np.asarray(x).astype(np.float64)


B, L, DIMIN, WIDTH, N_HEADS, N_EMBDS = 8, 128, 512, 2048, 8, 64
EPS = 1e-6
XS = 10.0
SD = np.sqrt(DIMIN / WIDTH)


def draw0():
    s = mx_kscale(WIDTH)
    t = mx_kscale(WIDTH)
    return {"o": bf(np.random.standard_normal((B, L, WIDTH)) * 0.6 * s),
            "o_w": bf(np.random.standard_normal((WIDTH, WIDTH)) * 0.5 / np.sqrt(WIDTH) / s[None, :] * t[:, None]),
            "o_b": bf(np.random.standard_normal(WIDTH) * 0.1 * t),
            "D": bf(np.random.standard_normal((WIDTH, DIMIN)) * SD / t[:, None]),
            "x": bf(np.random.standard_normal((B, L, DIMIN)) * XS)}


def core(o, o_w, o_b, D, x):
    xc = f64(x)
    d_target = (mxq(f64(o), 2, "e4m3") @ mxq(f64(o_w), 1, "e4m3").T) + f64(o_b)
    z_pred_ = np.maximum(d_target, 0.0)
    Dz = mxq(z_pred_, 2, "e4m3") @ mxq(f64(D), 0, "e4m3")
    Dz_norm = np.sqrt(np.sum(Dz * Dz, axis=-1, keepdims=True)) + EPS
    proj_scale = np.sum(Dz * xc, axis=-1, keepdims=True) / np.square(Dz_norm)
    z_pred = z_pred_ * proj_scale
    x_pred = proj_scale * Dz
    return z_pred, x_pred


def e4m3fn_bytes(y):
    return np.clip(np.asarray(y, np.float64), -448.0, 448.0).astype(np.float32).astype(ml_dtypes.float8_e4m3fn).view(np.uint8)


def e4m3fn_values(b):
    return np.asarray(b, np.uint8).view(ml_dtypes.float8_e4m3fn).astype(np.float64)


def setup_inputs():
    d = draw0()
    x0 = np.asarray(d['o']).astype(np.float64)
    s = (np.max(np.abs(x0), axis=(0, 1), keepdims=True) / 448.0).astype(np.float32)
    out = {}
    for k, v in d.items():
        if k == 'o':
            out['o_bytes'] = e4m3fn_bytes(x0 / s.astype(np.float64))
            out['o_scale'] = s
        else:
            out[k] = v
    return out


def reference(o_bytes, o_scale, o_w, o_b, D, x):
    return core(e4m3fn_values(o_bytes) * o_scale.astype(np.float64), o_w, o_b, D, x)

from contextlib import ExitStack

import concourse.mybir as mybir
from concourse.masks import make_identity

TOKENS, K, N, DIM = 1024, 2048, 2048, 512
EPS = 1e-6
FLOPS = 2 * TOKENS * K * N + 2 * TOKENS * N * DIM

F32 = mybir.dt.float32
BF16 = mybir.dt.bfloat16
U32 = mybir.dt.uint32
U8 = mybir.dt.uint8
FP8 = mybir.dt.float8_e4m3fn
FP8X4 = mybir.dt.float8_e4m3fn_x4
ALU = mybir.AluOpType
ACT = mybir.ActivationFunctionType
ENG = mybir.EngineType

P = 128
PASSES = K // 512
MT = TOKENS // P
NB = N // 512
WT = N // P
W_AHEAD = 5


def tile_originaltemporalsae_pa_kernel(tc, o_bytes, o_scale, o_w, o_b, D, x, out_0, out_1):
    nc = tc.nc
    with ExitStack() as ctx:
        const = ctx.enter_context(tc.tile_pool(name="const", bufs=1))
        keep = ctx.enter_context(tc.tile_pool(name="keep", bufs=1))
        io = ctx.enter_context(tc.tile_pool(name="io", bufs=2))
        work = ctx.enter_context(tc.tile_pool(name="work", bufs=2))
        ps_t = ctx.enter_context(tc.psum_pool(name="ps_t", bufs=4))
        ps_d = ctx.enter_context(tc.psum_pool(name="ps_d", bufs=3))
        ps_z = ctx.enter_context(tc.psum_pool(name="ps_z", bufs=1))

        ident = const.tile([P, P], F32, name="ident")
        make_identity(nc, ident[:])
        warm = const.tile([P, 1], F32, name="warm")
        nc.vector.memset(warm[:], 1.0)
        eps = const.tile([P, 1], F32, name="eps")
        nc.vector.tensor_scalar(out=eps[:], in0=warm[:], scalar1=EPS, scalar2=None, op0=ALU.mult)
        table = const.tile([P, 1], F32, name="table")
        nc.scalar.activation(out=table[:], in_=warm[:], func=ACT.Sqrt)

        scale = const.tile([P, K], F32, name="scale", align_bytes=64)
        bias = const.tile([P, N], BF16, name="bias", align_bytes=64)
        w_codes = [keep.tile([P, PASSES, 512], U32, name=f"wc{n}", align_bytes=64) for n in range(NB)]
        w_scales = [keep.tile([P, PASSES, 512], U8, name=f"ws{n}", align_bytes=64) for n in range(NB)]
        d_codes = [keep.tile([P, DIM], U32, name=f"dc{g}", align_bytes=64) for g in range(PASSES)]
        d_scales = [keep.tile([P, DIM], U8, name=f"ds{g}", align_bytes=64) for g in range(PASSES)]
        o_raw = [keep.tile([P, K], U8, name=f"oraw{m}", align_bytes=64) for m in range(MT)]

        w_raw, w_grp, o_bf, o_cod, r_cod = {}, {}, {}, {}, {}
        dd, r_bf, o_grp, r_grp, dz, stat = {}, {}, {}, {}, {}, {}
        d_raw, x_sb = {}, {}

        def load_w(j):
            t = io.tile([P, K], BF16, name="w_raw", bufs=W_AHEAD + 1, align_bytes=64)
            parts = 2 if j == 0 else 1
            for i in range(parts):
                cs = slice(K // parts * i, K // parts * (i + 1))
                nc.sync.dma_start(out=t[:, cs], in_=o_w[j * P:(j + 1) * P, cs])
            w_raw[j] = t

        def load_o(m):
            nc.sync.dma_start(out=o_raw[m][:], in_=o_bytes[m])

        def load_d(g):
            t = io.tile([P, 4, DIM], BF16, name="d_raw", bufs=2, align_bytes=64)
            nc.sync.dma_start(out=t[:], in_=D[g * 512:(g + 1) * 512, :].rearrange("(p j) n -> p j n", j=4))
            d_raw[g] = t

        def load_x(m):
            t = io.tile([P, DIM], BF16, name="x_sb", bufs=4, align_bytes=64)
            nc.sync.dma_start(out=t[:], in_=x[m])
            x_sb[m] = t

        def transpose_half(words, h, every_second):
            pt = ps_t.tile([P, 2, 2, P], F32, name="pt")
            for gg in range(2):
                for u in range(2):
                    base = 256 * (2 * h + gg)
                    if every_second:
                        src = words[:, base + u:base + 256:2]
                    else:
                        src = words[:, base + 128 * u:base + 128 * (u + 1)]
                    nc.tensor.transpose(pt[:, gg, u, :], src, ident[:])
            return pt

        def trans_w(j):
            n, r = divmod(j, 4)
            if r == 0:
                w_grp[n] = [work.tile([P, 2, 2048], BF16, name="big8", bufs=6, align_bytes=64) for h in range(2)]
            words = w_raw.pop(j)[:].bitcast(F32)
            for h in range(2):
                pt = transpose_half(words, h, True)
                dst = w_grp[n][h][:].bitcast(F32)[:, :, 256 * r:256 * (r + 1)].rearrange("p g (r u) -> p g r u", u=2)
                nc.scalar.copy(out=dst, in_=pt[:].rearrange("p g u r -> p g r u"))

        def quant_w(n):
            for g in range(PASSES):
                nc.vector.quantize_mx(
                    out=w_codes[n][:, g, :].bitcast(FP8X4), scales=w_scales[n][:, g, :],
                    in_=w_grp[n][g // 2][:, g % 2, :])

        def product(m, c):
            if m >= MT:
                return
            if c == 0:
                o_bf[m] = work.tile([P, K], BF16, name="o_bf", bufs=4, align_bytes=64)
            cs = slice(512 * c, 512 * (c + 1))
            nc.vector.tensor_tensor(out=o_bf[m][:, cs], in0=o_raw[m][:, cs].bitcast(FP8), in1=scale[:, cs], op=ALU.mult)

        def evac_half(pt, grp, h):
            dst = grp[:].bitcast(F32)[:, 512 * h:512 * (h + 1)].rearrange("p (g r u) -> p g r u", g=2, u=2)
            nc.scalar.copy(out=dst, in_=pt[:].rearrange("p g u r -> p g r u"))

        def trans_o(m):
            grp = work.tile([P, 2048], BF16, name="o_grp", bufs=2, align_bytes=64)
            words = o_bf.pop(m)[:].bitcast(F32)
            for h in range(2):
                evac_half(transpose_half(words, h, True), grp, h)
            o_grp[m] = grp

        def quant_o(m):
            c = work.tile([P, 512], U32, name="o_cod", bufs=2, align_bytes=64)
            s = work.tile([P, 512], U8, name="o_sca", bufs=2, align_bytes=64)
            nc.vector.quantize_mx(out=c[:].bitcast(FP8X4), scales=s[:], in_=o_grp.pop(m)[:])
            o_cod[m] = (c, s)

        def trans_r(m, h):
            if h == 0:
                r_grp[m] = work.tile([P, 2048], BF16, name="r_grp", bufs=2, align_bytes=64)
            evac_half(transpose_half(r_bf[m][:].bitcast(F32), h, False), r_grp[m], h)

        def quant_r(m, h):
            if h == 0:
                r_cod[m] = (work.tile([P, 512], U32, name="r_cod", bufs=2, align_bytes=64),
                            work.tile([P, 512], U8, name="r_sca", bufs=2, align_bytes=64))
            c, s = r_cod[m]
            cs = slice(256 * h, 256 * (h + 1))
            nc.vector.quantize_mx(out=c[:, cs].bitcast(FP8X4), scales=s[:, cs], in_=r_grp[m][:, 1024 * h:1024 * (h + 1)])

        def mx1(m, n):
            pd = ps_d.tile([P, 512], F32, name="pd")
            c, s = o_cod[m]
            for g in range(PASSES):
                gs = slice(P * g, P * (g + 1))
                nc.tensor.matmul_mx(out=pd[:], lhsT=c[:, gs].bitcast(FP8X4), lhsT_scale=s[:, gs],
                                    rhs=w_codes[n][:, g, :].bitcast(FP8X4), rhs_scale=w_scales[n][:, g, :],
                                    start=(g == 0), stop=(g == PASSES - 1))
            if n == 0:
                dd[m] = work.tile([P, 2048], F32, name="big8", bufs=6, align_bytes=64)
                r_bf[m] = work.tile([P, 2048], BF16, name="r_bf", bufs=2, align_bytes=64)
            ns = slice(512 * n, 512 * (n + 1))
            nc.vector.tensor_tensor(out=dd[m][:, ns], in0=pd[:], in1=bias[:, ns], op=ALU.add)
            nc.scalar.activation(
                out=r_bf[m][:, ns].rearrange("p (u q e) -> p u q e", u=2, e=2),
                in_=dd[m][:, ns].rearrange("p (q u e) -> p u q e", u=2, e=2), func=ACT.Relu)

        def mx2(m):
            z = ps_z.tile([P, DIM], F32, name="pz")
            c, s = r_cod.pop(m)
            for g in range(PASSES):
                gs = slice(P * g, P * (g + 1))
                nc.tensor.matmul_mx(out=z[:], lhsT=c[:, gs].bitcast(FP8X4), lhsT_scale=s[:, gs],
                                    rhs=d_codes[g][:].bitcast(FP8X4), rhs_scale=d_scales[g][:],
                                    start=(g == 0), stop=(g == PASSES - 1))
            dz[m] = z

        def sums(m):
            ssq = work.tile([P, 1], F32, name="ssq")
            dot = work.tile([P, 1], F32, name="dot")
            root = work.tile([P, 1], F32, name="root")
            nsq = work.tile([P, 1], F32, name="nsq")
            sq = work.tile([P, DIM], F32, name="sq", bufs=1)
            pr = work.tile([P, DIM], F32, name="pr", bufs=1)
            nc.scalar.activation(out=sq[:], in_=dz[m][:], func=ACT.Square, accum_out=ssq[:])
            nc.vector.scalar_tensor_tensor(out=pr[:], in0=dz[m][:], scalar=1.0, in1=x_sb.pop(m)[:],
                                           op0=ALU.mult, op1=ALU.mult, accum_out=dot[:])
            nc.scalar.activation(out=root[:], in_=ssq[:], func=ACT.Sqrt)
            nc.scalar.activation(out=nsq[:], in_=root[:], func=ACT.Square, bias=eps[:])
            stat[m] = (dot, nsq)

        def inverse(m):
            dot, nsq = stat[m]
            inv = work.tile([P, 1], F32, name="inv")
            nc.vector.reciprocal(inv[:], nsq[:])
            stat[m] = (dot, inv)

        def factor(m):
            dot, inv = stat[m]
            fac = work.tile([P, 1], F32, name="fac")
            nc.vector.tensor_tensor(out=fac[:], in0=dot[:], in1=inv[:], op=ALU.mult)
            stat[m] = fac

        def x_pred(m):
            xp = work.tile([P, DIM], F32, name="xp")
            nc.scalar.activation(out=xp[:], in_=dz.pop(m)[:], func=ACT.Copy, scale=stat[m][:])
            nc.sync.dma_start(out=out_1[m], in_=xp[:])

        def z_pred(m, i, pieces):
            w = 2048 // pieces
            cs = slice(w * i, w * (i + 1))
            nc.vector.tensor_scalar(out=dd[m][:, cs], in0=dd[m][:, cs], scalar1=0.0, scalar2=stat[m][:],
                                    op0=ALU.max, op1=ALU.mult)
            nc.sync.dma_start(out=out_0[m][:, cs], in_=dd[m][:, cs])

        def group_d(g, on_scalar):
            t = work.tile([P, DIM, 4], BF16, name="d_grp", bufs=2, align_bytes=64)
            src = d_raw.pop(g)[:].rearrange("p j n -> p n j")
            if on_scalar:
                nc.scalar.copy(out=t[:], in_=src)
            else:
                nc.vector.tensor_copy(out=t[:], in_=src)
            return t

        def quant_d(g, t):
            nc.vector.quantize_mx(out=d_codes[g][:].bitcast(FP8X4), scales=d_scales[g][:], in_=t[:].rearrange("p n j -> p (n j)"))

        def load_bias():
            nc.sync.dma_start(out=bias[:], in_=o_b.partition_broadcast(P))

        def load_scale():
            nc.sync.dma_start(out=scale[:], in_=o_scale.rearrange("a b k -> (a b k)").partition_broadcast(P))

        def products(m):
            for c in range(4):
                product(m, c)

        dt = {}

        def dgroup(g, on_scalar):
            dt[g] = group_d(g, on_scalar)

        def dquant(g):
            quant_d(g, dt.pop(g))

        for j in range(4):
            load_w(j)
        load_o(0)
        load_scale()
        load_w(4)
        load_w(5)
        plan = {
            0: [lambda: load_w(6)],
            1: [lambda: load_w(7)],
            2: [lambda: load_w(8), lambda: load_o(1)],
            3: [lambda: load_w(9), lambda: products(0), lambda: quant_w(0)],
            4: [lambda: load_w(10)],
            5: [lambda: load_w(11), lambda: load_o(2), lambda: trans_o(0), lambda: products(1), lambda: load_bias()],
            6: [lambda: load_w(12), lambda: quant_o(0)],
            7: [lambda: load_w(13), lambda: quant_w(1)],
            8: [lambda: load_w(14), lambda: load_o(3), lambda: mx1(0, 0)],
            9: [lambda: load_w(15), lambda: load_x(0), lambda: load_d(0), lambda: products(2)],
            10: [lambda: load_d(1)],
            11: [lambda: mx1(0, 1), lambda: quant_w(2)],
            12: [lambda: trans_o(1)],
            13: [lambda: products(3), lambda: dgroup(0, False)],
            14: [lambda: quant_o(1), lambda: load_d(2)],
            15: [lambda: mx1(0, 2), lambda: dquant(0), lambda: quant_w(3), lambda: dgroup(1, False), lambda: load_d(3),
                 lambda: mx1(1, 0), lambda: mx1(1, 1), lambda: mx1(0, 3)],
        }
        for j in range(WT):
            trans_w(j)
            for f in plan[j]:
                f()
        load_o(4)
        load_x(1)
        load_o(5)

        for m in range(1, MT):
            last = m == MT - 1
            if m + 5 < MT:
                load_o(m + 5)
            if m + 1 < MT:
                load_x(m + 1)
            if m >= 2:
                sums(m - 2)
            if not last:
                trans_o(m + 1)
            for h in range(2):
                trans_r(m - 1, h)
            product(m + 3, 0)
            if m >= 2:
                inverse(m - 2)
            product(m + 3, 1)
            if m >= 2:
                factor(m - 2)
                x_pred(m - 2)
            if m == 1:
                dquant(1)
                dgroup(2, True)
            quant_r(m - 1, 0)
            quant_r(m - 1, 1)
            if m >= 2:
                z_pred(m - 2, 0, 2)
            if m > 1:
                mx1(m, 0)
            if m == 1:
                dgroup(3, False)
            if not last:
                quant_o(m + 1)
            if m >= 2:
                z_pred(m - 2, 1, 2)
            if m > 1:
                mx1(m, 1)
            product(m + 3, 2)
            if last:
                mx2(m - 1)
                sums(m - 1)
            mx1(m, 2)
            product(m + 3, 3)
            if m == 1:
                dquant(2)
                dquant(3)
            if last:
                inverse(m - 1)
                trans_r(m, 0)
                factor(m - 1)
                quant_r(m, 0)
                x_pred(m - 1)
            mx1(m, 3)
            if last:
                z_pred(m - 1, 0, 2)
                z_pred(m - 1, 1, 2)
                trans_r(m, 1)
                quant_r(m, 1)
            mx2(m if last else m - 1)
        sums(MT - 1)
        inverse(MT - 1)
        factor(MT - 1)
        for i in range(4):
            z_pred(MT - 1, i, 4)
        x_pred(MT - 1)
